import numpy as np
import ml_dtypes


def mxq(x, axis, fmt="e4m3"):
    dtype, down = {"e4m3": (ml_dtypes.float8_e4m3fn, 7), "e5m2": (ml_dtypes.float8_e5m2, 14)}[fmt]
    v = np.moveaxis(np.asarray(x, np.float32).astype(ml_dtypes.bfloat16).astype(np.float64), axis, -1)
    blocks = v.reshape(v.shape[:-1] + (-1, 32))
    amax = np.abs(blocks).max(-1, keepdims=True)
    byte = np.maximum(np.where(amax > 0, np.frexp(amax)[1] - 1 + 127, 0) - down, 1)
    scale = np.exp2(byte - 127.0)
    codes = (blocks / scale).astype(np.float32).astype(dtype).astype(np.float64)
    return np.moveaxis((codes * scale).reshape(v.shape), -1, axis)


WIDE = False


def mx_kscale(k):
    if not WIDE:
        return np.ones(k)
    levels = np.array([10, -10, 5, -5, 0])
    a = np.random.permutation(np.resize(levels, k // 512 * 4)).reshape(k // 512, 4)
    idx = np.arange(k)
    return np.exp2(a[idx // 512, idx % 128 // 32])


BF16 = ml_dtypes.bfloat16


def bf(x):
    return np.asarray(x, np.float32).astype(BF16)


def f64(x):
    return np.asarray(x).astype(np.float64)


B, T, P, F, G, R, C, O = 16, 8, 512, 512, 512, 128, 4, 10


def setup_inputs():
    s, t = mx_kscale(P + F), mx_kscale(G)
    u = np.roll(t, R)
    r0 = np.concatenate([1.0 / (np.sqrt(P + F) * s), [0.1]])[:, None]
    r1 = np.concatenate([1.5 / (np.sqrt(G) * t), [0.1]])[:, None]
    return {"primary_input": bf((np.random.standard_normal((B, T, P)) * s[:P]).reshape(B, T * P)),
            "prev": bf((np.maximum(np.random.standard_normal((B, T, F)), 0.0) * 0.9 * s[P:]).reshape(B, T * F)),
            "col": bf(np.array([float(np.random.randint(1, C))])),
            "W0": bf(np.random.standard_normal((P + F + 1, G)) * r0 * u),
            "b0": bf(np.random.standard_normal(G) * 0.2 * u),
            "W1": bf(np.random.standard_normal((G + 1, F)) * r1),
            "b1": bf(np.random.standard_normal(F) * 0.2)}


def reference(primary_input, prev, col, W0, b0, W1, b1):
    w0, w1, c = f64(W0), f64(W1), f64(col)
    inp = np.concatenate([f64(primary_input).reshape(B, T, P), f64(prev).reshape(B, T, F)], axis=-1)
    a = (mxq(inp, 2, "e4m3") @ mxq(w0[:P + F], 0, "e4m3")) + c * w0[P + F] + f64(b0)
    h = np.roll(np.maximum(a, 0.0).reshape(B, T * G), -R, axis=1).reshape(B, T, G)
    y = (mxq(h, 2, "e4m3") @ mxq(w1[:G], 0, "e4m3")) + c * w1[G] + f64(b1)
    return np.roll(np.maximum(y, 0.0).reshape(B, T * F), R, axis=1)

@@ -1,0 +1,205 @@
+import concourse.mybir as mybir
+from concourse.masks import make_identity
+
+BF16 = mybir.dt.bfloat16
+F32 = mybir.dt.float32
+U32 = mybir.dt.uint32
+U8 = mybir.dt.uint8
+FP8X4 = mybir.dt.float8_e4m3fn_x4
+ADD = mybir.AluOpType.add
+MAX = mybir.AluOpType.max
+RELU = mybir.ActivationFunctionType.Relu
+
+P = 128
+PACK = 4
+K_PASS = P * PACK
+T = 8
+WIDTH = 512
+ROLL = 128
+HALF = WIDTH // 2
+QUARTER = WIDTH // 4
+L1_PASSES = 2
+CHUNKS = WIDTH // P
+
+FLOPS = 2 * P * (L1_PASSES * K_PASS) * WIDTH + 2 * P * K_PASS * WIDTH
+
+
+def regroup(copy, grouped, raw, cols):
+    copy(
+        out=grouped[:, cols, :].rearrange("p (c i) j -> p c j i", i=4),
+        in_=raw[:, :, cols].rearrange("p j (c i) -> p c j i", i=4),
+    )
+
+
+def quantise(nc, codes, scales, grouped):
+    nc.vector.quantize_mx(
+        out=codes.bitcast(FP8X4),
+        scales=scales,
+        in_=grouped.rearrange("p w j -> p (w j)"),
+    )
+
+
+def tile_capsuleneuralnetwork_pa_s_kernel(tc, primary_input, prev, col, W0, b0, W1, b1, out):
+    nc = tc.nc
+    lo = slice(0, HALF)
+    hi = slice(HALF, WIDTH)
+    quarters = [slice(q * QUARTER, (q + 1) * QUARTER) for q in range(4)]
+
+    with tc.tile_pool(name="keep", bufs=1) as keep, tc.psum_pool(name="psum", bufs=1) as psum, tc.manual_schedule():
+        x_sb = keep.tile([P, L1_PASSES * K_PASS], BF16)
+        x_grouped = keep.tile([P, L1_PASSES * P * PACK], BF16, align_bytes=64)
+        x_codes = keep.tile([P, L1_PASSES, P], U32, align_bytes=64)
+        x_scales = keep.tile([P, L1_PASSES, P], U8, align_bytes=64)
+        w0_raw = keep.tile([P, L1_PASSES, PACK, WIDTH], BF16)
+        w0_grouped = keep.tile([P, L1_PASSES, WIDTH, PACK], BF16, align_bytes=64)
+        w0_codes = keep.tile([P, L1_PASSES, WIDTH], U32, align_bytes=64)
+        w0_scales = keep.tile([P, L1_PASSES, WIDTH], U8, align_bytes=64)
+        w1_raw = keep.tile([P, PACK, WIDTH], BF16)
+        w1_grouped = keep.tile([P, WIDTH, PACK], BF16, align_bytes=64)
+        w1_codes = keep.tile([P, WIDTH], U32, align_bytes=64)
+        w1_scales = keep.tile([P, WIDTH], U8, align_bytes=64)
+        h_planes = keep.tile([P, PACK, P], BF16)
+        h_grouped = keep.tile([P, P, PACK], BF16, align_bytes=64)
+        h_codes = keep.tile([P, P], U32, align_bytes=64)
+        h_scales = keep.tile([P, P], U8, align_bytes=64)
+        ident = keep.tile([P, P], F32)
+        bias_rows = keep.tile([P, 2, WIDTH], BF16)
+        weight_of_row = keep.tile([P, 1], BF16)
+        bias0 = keep.tile([P, CHUNKS], F32)
+        bias1 = keep.tile([P, WIDTH], F32)
+        y_sum = keep.tile([P, WIDTH], F32)
+        y_out = keep.tile([P, WIDTH], F32)
+
+        xt = [psum.tile([P, 2, P], F32, name="xt%d" % g, tag="bank%d" % g) for g in range(L1_PASSES)]
+        bias0_ps = psum.tile([P, CHUNKS], F32)
+        bias1_ps = psum.tile([P, WIDTH], F32)
+        a_ps = [psum.tile([P, P], F32, name="a_ps%d" % c) for c in range(CHUNKS)]
+
+        nc.vector.memset(bias_rows[:], 0.0)
+        nc.vector.memset(weight_of_row[:], 0.0)
+        nc.vector.memset(weight_of_row[0:1, :], 1.0)
+        make_identity(nc, ident[:])
+
+        nc.scalar.dma_start(out=weight_of_row[1:2, :], in_=col.unsqueeze(0))
+        nc.scalar.dma_start(out=bias_rows[0:1, 0, :], in_=b0.unsqueeze(0))
+        nc.scalar.dma_start(out=bias_rows[1:2, 0, :], in_=W0[L1_PASSES * K_PASS : L1_PASSES * K_PASS + 1, :])
+        nc.scalar.dma_start(out=bias_rows[0:1, 1, :], in_=b1.unsqueeze(0))
+        nc.scalar.dma_start(out=bias_rows[1:2, 1, :], in_=W1[K_PASS : K_PASS + 1, :])
+
+        nc.sync.dma_start(out=x_sb[:, 0:K_PASS], in_=primary_input.rearrange("b (t k) -> (b t) k", k=K_PASS))
+        nc.sync.dma_start(out=x_sb[:, K_PASS : 2 * K_PASS], in_=prev.rearrange("b (t k) -> (b t) k", k=K_PASS))
+        for g in range(L1_PASSES):
+            nc.sync.dma_start(
+                out=w0_raw[:, g],
+                in_=W0[g * K_PASS : (g + 1) * K_PASS, :].rearrange("(p j) w -> p j w", j=PACK),
+            )
+        nc.sync.dma_start(out=w1_raw[:], in_=W1[0:K_PASS, :].rearrange("(j p) w -> p j w", p=P))
+
+
+        x_words = x_sb[:].bitcast(F32).rearrange("r (g p u) -> r g u p", g=L1_PASSES, u=2)
+        x_grouped_words = x_grouped[:].bitcast(F32).rearrange("p (g r u) -> p g r u", g=L1_PASSES, u=2)
+        for g in range(L1_PASSES):
+            for u in range(2):
+                nc.tensor.transpose(out=xt[g][:, u, :], in_=x_words[:, g, u, :], identity=ident[:])
+        nc.vector.tensor_copy(out=x_grouped_words[:, 0], in_=xt[0][:].rearrange("p u r -> p r u"))
+        nc.scalar.copy(out=x_grouped_words[:, 1], in_=xt[1][:].rearrange("p u r -> p r u"))
+
+        for c in range(CHUNKS):
+            nc.tensor.matmul(
+                out=bias0_ps[:, c : c + 1],
+                lhsT=bias_rows[:, 0, c * P : (c + 1) * P],
+                rhs=weight_of_row[:],
+                start=True,
+                stop=True,
+            )
+        nc.tensor.matmul(
+            out=bias1_ps[:],
+            lhsT=weight_of_row[:].to_broadcast([P, P]),
+            rhs=bias_rows[:, 1, :],
+            start=True,
+            stop=True,
+        )
+        nc.vector.tensor_copy(out=bias0[:], in_=bias0_ps[:])
+        nc.scalar.copy(out=bias1[:], in_=bias1_ps[:])
+
+        def layer1(g, chunks):
+            for c in chunks:
+                cols = slice(c * P, (c + 1) * P)
+                nc.tensor.matmul_mx(
+                    out=a_ps[c][:],
+                    lhsT=w0_codes[:, g, cols].bitcast(FP8X4),
+                    lhsT_scale=w0_scales[:, g, cols],
+                    rhs=x_codes[:, g, :].bitcast(FP8X4),
+                    rhs_scale=x_scales[:, g, :],
+                    start=(g == 0),
+                    stop=(g == L1_PASSES - 1),
+                )
+
+        def quantise_w0(g, cols):
+            quantise(nc, w0_codes[:, g, cols], w0_scales[:, g, cols], w0_grouped[:, g, cols, :])
+
+        regroup(nc.vector.tensor_copy, w0_grouped[:, 0], w0_raw[:, 0], lo)
+        regroup(nc.scalar.copy, w0_grouped[:, 0], w0_raw[:, 0], quarters[2])
+        regroup(nc.scalar.copy, w0_grouped[:, 0], w0_raw[:, 0], quarters[3])
+        nc.vector.quantize_mx(
+            out=x_codes[:].rearrange("p g r -> p (g r)").bitcast(FP8X4),
+            scales=x_scales[:].rearrange("p g r -> p (g r)"),
+            in_=x_grouped[:],
+        )
+        quantise_w0(0, lo)
+        layer1(0, (0, 1))
+        regroup(nc.vector.tensor_copy, w0_grouped[:, 1], w0_raw[:, 1], lo)
+        regroup(nc.scalar.copy, w0_grouped[:, 1], w0_raw[:, 1], quarters[2])
+        regroup(nc.scalar.copy, w0_grouped[:, 1], w0_raw[:, 1], quarters[3])
+        quantise_w0(0, hi)
+        layer1(0, (2, 3))
+        quantise_w0(1, lo)
+        layer1(1, (0, 1))
+        quantise_w0(1, hi)
+        layer1(1, (2, 3))
+
+        regroup(nc.scalar.copy, w1_grouped, w1_raw, quarters[0])
+        a0_rows = a_ps[0][:].rearrange("p (b t) -> p b t", t=T)
+        h3_rows = h_planes[:, 3, :].rearrange("p (b t) -> p b t", t=T)
+        nc.vector.tensor_scalar(
+            out=h3_rows[:, :, 0 : T - 1], in0=a0_rows[:, :, 1:T], scalar1=bias0[:, 0:1], scalar2=0.0, op0=ADD, op1=MAX
+        )
+        nc.vector.tensor_scalar(
+            out=h3_rows[:, :, T - 1 : T], in0=a0_rows[:, :, 0:1], scalar1=bias0[:, 0:1], scalar2=0.0, op0=ADD, op1=MAX
+        )
+        nc.vector.tensor_scalar(
+            out=h_planes[:, 0, :], in0=a_ps[1][:], scalar1=bias0[:, 1:2], scalar2=0.0, op0=ADD, op1=MAX
+        )
+        for c in (2, 3):
+            nc.scalar.activation(out=h_planes[:, c - 1, :], in_=a_ps[c][:], func=RELU, bias=bias0[:, c : c + 1], scale=1.0)
+        regroup(nc.scalar.copy, w1_grouped, w1_raw, quarters[1])
+        regroup(nc.vector.tensor_copy, w1_grouped, w1_raw, hi)
+        nc.vector.tensor_copy(out=h_grouped[:], in_=h_planes[:].rearrange("p j r -> p r j"))
+        quantise(nc, w1_codes[:, hi], w1_scales[:, hi], w1_grouped[:, hi, :])
+        quantise(nc, h_codes[:], h_scales[:], h_grouped[:])
+        quantise(nc, w1_codes[:, lo], w1_scales[:, lo], w1_grouped[:, lo, :])
+
+        out_rows = out.rearrange("b (t f) -> (b t) f", f=WIDTH)
+        y_ps = {}
+        for n, cols in enumerate((hi, lo)):
+            y_ps[n] = psum.tile([P, HALF], F32, name="y_ps%d" % n, tag="bank%d" % n)
+            nc.tensor.matmul_mx(
+                out=y_ps[n][:],
+                lhsT=h_codes[:].bitcast(FP8X4),
+                lhsT_scale=h_scales[:],
+                rhs=w1_codes[:, cols].bitcast(FP8X4),
+                rhs_scale=w1_scales[:, cols],
+                start=True,
+                stop=True,
+            )
+            nc.vector.tensor_tensor(out=y_sum[:, cols], in0=y_ps[n][:], in1=bias1[:, cols], op=ADD)
+            nc.scalar.activation(out=y_out[:, cols], in_=y_sum[:, cols], func=RELU)
+            if n == 0:
+                last = slice(WIDTH - ROLL, WIDTH)
+                for step in (2, 4, 8):
+                    first = step // 2 - 1
+                    nc.sync.dma_start(out=out_rows[first + 1 : P : step, 0:ROLL], in_=y_out[first:P:step, last])
+                nc.sync.dma_start(out=out_rows[0:P:T, 0:ROLL], in_=y_out[T - 1 : P : T, last])
+                nc.sync.dma_start(out=out_rows[:, HALF + ROLL : WIDTH], in_=y_out[:, HALF : WIDTH - ROLL])
+            else:
+                nc.sync.dma_start(out=out_rows[:, ROLL : HALF + ROLL], in_=y_out[:, lo])

@@ -69,12 +69,14 @@ def tile_capsuleneuralnetwork_pa_s_kernel(tc, primary_input, prev, col, W0, b0, 
         bias1 = keep.tile([P, WIDTH], F32)
         y_sum = keep.tile([P, WIDTH], F32)
         y_out = keep.tile([P, WIDTH], F32)
+        warm = keep.tile([P, 1], F32)
 
         xt = [psum.tile([P, 2, P], F32, name="xt%d" % g, tag="bank%d" % g) for g in range(L1_PASSES)]
         bias0_ps = psum.tile([P, CHUNKS], F32)
         bias1_ps = psum.tile([P, WIDTH], F32)
         a_ps = [psum.tile([P, P], F32, name="a_ps%d" % c) for c in range(CHUNKS)]
 
+        nc.vector.memset(warm[:], 0.0)
         nc.vector.memset(bias_rows[:], 0.0)
         nc.vector.memset(weight_of_row[:], 0.0)
         nc.vector.memset(weight_of_row[0:1, :], 1.0)
@@ -85,6 +87,7 @@ def tile_capsuleneuralnetwork_pa_s_kernel(tc, primary_input, prev, col, W0, b0, 
         nc.scalar.dma_start(out=bias_rows[1:2, 0, :], in_=W0[L1_PASSES * K_PASS : L1_PASSES * K_PASS + 1, :])
         nc.scalar.dma_start(out=bias_rows[0:1, 1, :], in_=b1.unsqueeze(0))
         nc.scalar.dma_start(out=bias_rows[1:2, 1, :], in_=W1[K_PASS : K_PASS + 1, :])
+        nc.scalar.activation(out=warm[:], in_=warm[:], func=RELU)
 
         nc.sync.dma_start(out=x_sb[:, 0:K_PASS], in_=primary_input.rearrange("b (t k) -> (b t) k", k=K_PASS))
         nc.sync.dma_start(out=x_sb[:, K_PASS : 2 * K_PASS], in_=prev.rearrange("b (t k) -> (b t) k", k=K_PASS))

@@ -76,17 +76,15 @@ def tile_capsuleneuralnetwork_pa_s_kernel(tc, primary_input, prev, col, W0, b0, 
         bias1_ps = psum.tile([P, WIDTH], F32)
         a_ps = [psum.tile([P, P], F32, name="a_ps%d" % c) for c in range(CHUNKS)]
 
-        nc.vector.memset(warm[:], 0.0)
-        nc.vector.memset(bias_rows[:], 0.0)
         nc.vector.memset(weight_of_row[:], 0.0)
         nc.vector.memset(weight_of_row[0:1, :], 1.0)
+        nc.vector.memset(bias_rows[:], 0.0)
+        nc.vector.memset(warm[:], 0.0)
         make_identity(nc, ident[:])
 
         nc.scalar.dma_start(out=weight_of_row[1:2, :], in_=col.unsqueeze(0))
         nc.scalar.dma_start(out=bias_rows[0:1, 0, :], in_=b0.unsqueeze(0))
         nc.scalar.dma_start(out=bias_rows[1:2, 0, :], in_=W0[L1_PASSES * K_PASS : L1_PASSES * K_PASS + 1, :])
-        nc.scalar.dma_start(out=bias_rows[0:1, 1, :], in_=b1.unsqueeze(0))
-        nc.scalar.dma_start(out=bias_rows[1:2, 1, :], in_=W1[K_PASS : K_PASS + 1, :])
         nc.scalar.activation(out=warm[:], in_=warm[:], func=RELU)
 
         nc.sync.dma_start(out=x_sb[:, 0:K_PASS], in_=primary_input.rearrange("b (t k) -> (b t) k", k=K_PASS))
@@ -97,6 +95,8 @@ def tile_capsuleneuralnetwork_pa_s_kernel(tc, primary_input, prev, col, W0, b0, 
                 in_=W0[g * K_PASS : (g + 1) * K_PASS, :].rearrange("(p j) w -> p j w", j=PACK),
             )
         nc.sync.dma_start(out=w1_raw[:], in_=W1[0:K_PASS, :].rearrange("(j p) w -> p j w", p=P))
+        nc.sync.dma_start(out=bias_rows[0:1, 1, :], in_=b1.unsqueeze(0))
+        nc.sync.dma_start(out=bias_rows[1:2, 1, :], in_=W1[K_PASS : K_PASS + 1, :])
 
 
         x_words = x_sb[:].bitcast(F32).rearrange("r (g p u) -> r g u p", g=L1_PASSES, u=2)
@@ -106,24 +106,6 @@ def tile_capsuleneuralnetwork_pa_s_kernel(tc, primary_input, prev, col, W0, b0, 
                 nc.tensor.transpose(out=xt[g][:, u, :], in_=x_words[:, g, u, :], identity=ident[:])
         nc.vector.tensor_copy(out=x_grouped_words[:, 0], in_=xt[0][:].rearrange("p u r -> p r u"))
         nc.scalar.copy(out=x_grouped_words[:, 1], in_=xt[1][:].rearrange("p u r -> p r u"))
-
-        for c in range(CHUNKS):
-            nc.tensor.matmul(
-                out=bias0_ps[:, c : c + 1],
-                lhsT=bias_rows[:, 0, c * P : (c + 1) * P],
-                rhs=weight_of_row[:],
-                start=True,
-                stop=True,
-            )
-        nc.tensor.matmul(
-            out=bias1_ps[:],
-            lhsT=weight_of_row[:].to_broadcast([P, P]),
-            rhs=bias_rows[:, 1, :],
-            start=True,
-            stop=True,
-        )
-        nc.vector.tensor_copy(out=bias0[:], in_=bias0_ps[:])
-        nc.scalar.copy(out=bias1[:], in_=bias1_ps[:])
 
         def layer1(g, chunks):
             for c in chunks:
@@ -156,10 +138,26 @@ def tile_capsuleneuralnetwork_pa_s_kernel(tc, primary_input, prev, col, W0, b0, 
         regroup(nc.scalar.copy, w0_grouped[:, 1], w0_raw[:, 1], quarters[3])
         quantise_w0(0, hi)
         layer1(0, (2, 3))
+        for c in range(CHUNKS):
+            nc.tensor.matmul(
+                out=bias0_ps[:, c : c + 1],
+                lhsT=bias_rows[:, 0, c * P : (c + 1) * P],
+                rhs=weight_of_row[:],
+                start=True,
+                stop=True,
+            )
         quantise_w0(1, lo)
         layer1(1, (0, 1))
         quantise_w0(1, hi)
         layer1(1, (2, 3))
+        nc.vector.tensor_copy(out=bias0[:], in_=bias0_ps[:])
+        nc.tensor.matmul(
+            out=bias1_ps[:],
+            lhsT=weight_of_row[:].to_broadcast([P, P]),
+            rhs=bias_rows[:, 1, :],
+            start=True,
+            stop=True,
+        )
 
         regroup(nc.scalar.copy, w1_grouped, w1_raw, quarters[0])
         a0_rows = a_ps[0][:].rearrange("p (b t) -> p b t", t=T)
@@ -176,6 +174,7 @@ def tile_capsuleneuralnetwork_pa_s_kernel(tc, primary_input, prev, col, W0, b0, 
         for c in (2, 3):
             nc.scalar.activation(out=h_planes[:, c - 1, :], in_=a_ps[c][:], func=RELU, bias=bias0[:, c : c + 1], scale=1.0)
         regroup(nc.scalar.copy, w1_grouped, w1_raw, quarters[1])
+        nc.scalar.copy(out=bias1[:], in_=bias1_ps[:])
         regroup(nc.vector.tensor_copy, w1_grouped, w1_raw, hi)
         nc.vector.tensor_copy(out=h_grouped[:], in_=h_planes[:].rearrange("p j r -> p r j"))
         quantise(nc, w1_codes[:, hi], w1_scales[:, hi], w1_grouped[:, hi, :])

@@ -17,17 +17,16 @@ T = 8
 WIDTH = 512
 ROLL = 128
 HALF = WIDTH // 2
-QUARTER = WIDTH // 4
 L1_PASSES = 2
 CHUNKS = WIDTH // P
 
 FLOPS = 2 * P * (L1_PASSES * K_PASS) * WIDTH + 2 * P * K_PASS * WIDTH
 
 
-def regroup(copy, grouped, raw, cols):
+def regroup(copy, grouped, raw, rows, cols):
     copy(
-        out=grouped[:, cols, :].rearrange("p (c i) j -> p c j i", i=4),
-        in_=raw[:, :, cols].rearrange("p j (c i) -> p c j i", i=4),
+        out=grouped[:, cols, rows].rearrange("p (c i) j -> p c j i", i=4),
+        in_=raw[:, rows, cols].rearrange("p j (c i) -> p c j i", i=4),
     )
 
 
@@ -43,7 +42,7 @@ def tile_capsuleneuralnetwork_pa_s_kernel(tc, primary_input, prev, col, W0, b0, 
     nc = tc.nc
     lo = slice(0, HALF)
     hi = slice(HALF, WIDTH)
-    quarters = [slice(q * QUARTER, (q + 1) * QUARTER) for q in range(4)]
+    row_pairs = (slice(0, 2), slice(2, PACK))
 
     with tc.tile_pool(name="keep", bufs=1) as keep, tc.psum_pool(name="psum", bufs=1) as psum, tc.manual_schedule():
         x_sb = keep.tile([P, L1_PASSES * K_PASS], BF16)
@@ -90,11 +89,12 @@ def tile_capsuleneuralnetwork_pa_s_kernel(tc, primary_input, prev, col, W0, b0, 
         nc.sync.dma_start(out=x_sb[:, 0:K_PASS], in_=primary_input.rearrange("b (t k) -> (b t) k", k=K_PASS))
         nc.sync.dma_start(out=x_sb[:, K_PASS : 2 * K_PASS], in_=prev.rearrange("b (t k) -> (b t) k", k=K_PASS))
         for g in range(L1_PASSES):
-            nc.sync.dma_start(
-                out=w0_raw[:, g],
-                in_=W0[g * K_PASS : (g + 1) * K_PASS, :].rearrange("(p j) w -> p j w", j=PACK),
-            )
-        nc.sync.dma_start(out=w1_raw[:], in_=W1[0:K_PASS, :].rearrange("(j p) w -> p j w", p=P))
+            w0_rows = W0[g * K_PASS : (g + 1) * K_PASS, :].rearrange("(p j) w -> p j w", j=PACK)
+            for rows in row_pairs:
+                nc.sync.dma_start(out=w0_raw[:, g, rows, :], in_=w0_rows[:, rows, :])
+        w1_rows = W1[0:K_PASS, :].rearrange("(j p) w -> p j w", p=P)
+        for rows in row_pairs:
+            nc.sync.dma_start(out=w1_raw[:, rows, :], in_=w1_rows[:, rows, :])
         nc.sync.dma_start(out=bias_rows[0:1, 1, :], in_=b1.unsqueeze(0))
         nc.sync.dma_start(out=bias_rows[1:2, 1, :], in_=W1[K_PASS : K_PASS + 1, :])
 
@@ -123,21 +123,23 @@ def tile_capsuleneuralnetwork_pa_s_kernel(tc, primary_input, prev, col, W0, b0, 
         def quantise_w0(g, cols):
             quantise(nc, w0_codes[:, g, cols], w0_scales[:, g, cols], w0_grouped[:, g, cols, :])
 
-        regroup(nc.vector.tensor_copy, w0_grouped[:, 0], w0_raw[:, 0], lo)
-        regroup(nc.scalar.copy, w0_grouped[:, 0], w0_raw[:, 0], quarters[2])
-        regroup(nc.scalar.copy, w0_grouped[:, 0], w0_raw[:, 0], quarters[3])
+        def regroup_w0(g, rows):
+            regroup(nc.vector.tensor_copy, w0_grouped[:, g], w0_raw[:, g], rows, lo)
+            regroup(nc.scalar.copy, w0_grouped[:, g], w0_raw[:, g], rows, hi)
+
+        regroup_w0(0, row_pairs[0])
         nc.vector.quantize_mx(
             out=x_codes[:].rearrange("p g r -> p (g r)").bitcast(FP8X4),
             scales=x_scales[:].rearrange("p g r -> p (g r)"),
             in_=x_grouped[:],
         )
+        regroup_w0(0, row_pairs[1])
         quantise_w0(0, lo)
         layer1(0, (0, 1))
-        regroup(nc.vector.tensor_copy, w0_grouped[:, 1], w0_raw[:, 1], lo)
-        regroup(nc.scalar.copy, w0_grouped[:, 1], w0_raw[:, 1], quarters[2])
-        regroup(nc.scalar.copy, w0_grouped[:, 1], w0_raw[:, 1], quarters[3])
+        regroup_w0(1, row_pairs[0])
         quantise_w0(0, hi)
         layer1(0, (2, 3))
+        regroup_w0(1, row_pairs[1])
         for c in range(CHUNKS):
             nc.tensor.matmul(
                 out=bias0_ps[:, c : c + 1],
@@ -159,7 +161,7 @@ def tile_capsuleneuralnetwork_pa_s_kernel(tc, primary_input, prev, col, W0, b0, 
             stop=True,
         )
 
-        regroup(nc.scalar.copy, w1_grouped, w1_raw, quarters[0])
+        regroup(nc.scalar.copy, w1_grouped, w1_raw, row_pairs[0], lo)
         a0_rows = a_ps[0][:].rearrange("p (b t) -> p b t", t=T)
         h3_rows = h_planes[:, 3, :].rearrange("p (b t) -> p b t", t=T)
         nc.vector.tensor_scalar(
@@ -173,9 +175,10 @@ def tile_capsuleneuralnetwork_pa_s_kernel(tc, primary_input, prev, col, W0, b0, 
         )
         for c in (2, 3):
             nc.scalar.activation(out=h_planes[:, c - 1, :], in_=a_ps[c][:], func=RELU, bias=bias0[:, c : c + 1], scale=1.0)
-        regroup(nc.scalar.copy, w1_grouped, w1_raw, quarters[1])
+        regroup(nc.scalar.copy, w1_grouped, w1_raw, row_pairs[1], lo)
         nc.scalar.copy(out=bias1[:], in_=bias1_ps[:])
-        regroup(nc.vector.tensor_copy, w1_grouped, w1_raw, hi)
+        for rows in row_pairs:
+            regroup(nc.vector.tensor_copy, w1_grouped, w1_raw, rows, hi)
         nc.vector.tensor_copy(out=h_grouped[:], in_=h_planes[:].rearrange("p j r -> p r j"))
         quantise(nc, w1_codes[:, hi], w1_scales[:, hi], w1_grouped[:, hi, :])
         quantise(nc, h_codes[:], h_scales[:], h_grouped[:])
@@ -204,4 +207,4 @@ def tile_capsuleneuralnetwork_pa_s_kernel(tc, primary_input, prev, col, W0, b0, 
                 nc.sync.dma_start(out=out_rows[0:P:T, 0:ROLL], in_=y_out[T - 1 : P : T, last])
                 nc.sync.dma_start(out=out_rows[:, HALF + ROLL : WIDTH], in_=y_out[:, HALF : WIDTH - ROLL])
             else:
-                nc.sync.dma_start(out=out_rows[:, ROLL : HALF + ROLL], in_=y_out[:, lo])
+                nc.scalar.dma_start(out=out_rows[:, ROLL : HALF + ROLL], in_=y_out[:, lo])

@@ -17,16 +17,17 @@ T = 8
 WIDTH = 512
 ROLL = 128
 HALF = WIDTH // 2
+QUARTER = WIDTH // 4
 L1_PASSES = 2
 CHUNKS = WIDTH // P
 
 FLOPS = 2 * P * (L1_PASSES * K_PASS) * WIDTH + 2 * P * K_PASS * WIDTH
 
 
-def regroup(copy, grouped, raw, rows, cols):
+def regroup(copy, grouped, raw, cols):
     copy(
-        out=grouped[:, cols, rows].rearrange("p (c i) j -> p c j i", i=4),
-        in_=raw[:, rows, cols].rearrange("p j (c i) -> p c j i", i=4),
+        out=grouped[:, cols, :].rearrange("p (c i) j -> p c j i", i=4),
+        in_=raw[:, :, cols].rearrange("p j (c i) -> p c j i", i=4),
     )
 
 
@@ -42,7 +43,7 @@ def tile_capsuleneuralnetwork_pa_s_kernel(tc, primary_input, prev, col, W0, b0, 
     nc = tc.nc
     lo = slice(0, HALF)
     hi = slice(HALF, WIDTH)
-    row_pairs = (slice(0, 2), slice(2, PACK))
+    quarters = [slice(q * QUARTER, (q + 1) * QUARTER) for q in range(4)]
 
     with tc.tile_pool(name="keep", bufs=1) as keep, tc.psum_pool(name="psum", bufs=1) as psum, tc.manual_schedule():
         x_sb = keep.tile([P, L1_PASSES * K_PASS], BF16)
@@ -89,12 +90,11 @@ def tile_capsuleneuralnetwork_pa_s_kernel(tc, primary_input, prev, col, W0, b0, 
         nc.sync.dma_start(out=x_sb[:, 0:K_PASS], in_=primary_input.rearrange("b (t k) -> (b t) k", k=K_PASS))
         nc.sync.dma_start(out=x_sb[:, K_PASS : 2 * K_PASS], in_=prev.rearrange("b (t k) -> (b t) k", k=K_PASS))
         for g in range(L1_PASSES):
-            w0_rows = W0[g * K_PASS : (g + 1) * K_PASS, :].rearrange("(p j) w -> p j w", j=PACK)
-            for rows in row_pairs:
-                nc.sync.dma_start(out=w0_raw[:, g, rows, :], in_=w0_rows[:, rows, :])
-        w1_rows = W1[0:K_PASS, :].rearrange("(j p) w -> p j w", p=P)
-        for rows in row_pairs:
-            nc.sync.dma_start(out=w1_raw[:, rows, :], in_=w1_rows[:, rows, :])
+            nc.sync.dma_start(
+                out=w0_raw[:, g],
+                in_=W0[g * K_PASS : (g + 1) * K_PASS, :].rearrange("(p j) w -> p j w", j=PACK),
+            )
+        nc.sync.dma_start(out=w1_raw[:], in_=W1[0:K_PASS, :].rearrange("(j p) w -> p j w", p=P))
         nc.sync.dma_start(out=bias_rows[0:1, 1, :], in_=b1.unsqueeze(0))
         nc.sync.dma_start(out=bias_rows[1:2, 1, :], in_=W1[K_PASS : K_PASS + 1, :])
 
@@ -123,23 +123,21 @@ def tile_capsuleneuralnetwork_pa_s_kernel(tc, primary_input, prev, col, W0, b0, 
         def quantise_w0(g, cols):
             quantise(nc, w0_codes[:, g, cols], w0_scales[:, g, cols], w0_grouped[:, g, cols, :])
 
-        def regroup_w0(g, rows):
-            regroup(nc.vector.tensor_copy, w0_grouped[:, g], w0_raw[:, g], rows, lo)
-            regroup(nc.scalar.copy, w0_grouped[:, g], w0_raw[:, g], rows, hi)
-
-        regroup_w0(0, row_pairs[0])
+        regroup(nc.vector.tensor_copy, w0_grouped[:, 0], w0_raw[:, 0], lo)
+        regroup(nc.scalar.copy, w0_grouped[:, 0], w0_raw[:, 0], quarters[2])
+        regroup(nc.scalar.copy, w0_grouped[:, 0], w0_raw[:, 0], quarters[3])
         nc.vector.quantize_mx(
             out=x_codes[:].rearrange("p g r -> p (g r)").bitcast(FP8X4),
             scales=x_scales[:].rearrange("p g r -> p (g r)"),
             in_=x_grouped[:],
         )
-        regroup_w0(0, row_pairs[1])
         quantise_w0(0, lo)
         layer1(0, (0, 1))
-        regroup_w0(1, row_pairs[0])
+        regroup(nc.vector.tensor_copy, w0_grouped[:, 1], w0_raw[:, 1], lo)
+        regroup(nc.scalar.copy, w0_grouped[:, 1], w0_raw[:, 1], quarters[2])
+        regroup(nc.scalar.copy, w0_grouped[:, 1], w0_raw[:, 1], quarters[3])
         quantise_w0(0, hi)
         layer1(0, (2, 3))
-        regroup_w0(1, row_pairs[1])
         for c in range(CHUNKS):
             nc.tensor.matmul(
                 out=bias0_ps[:, c : c + 1],
@@ -161,7 +159,7 @@ def tile_capsuleneuralnetwork_pa_s_kernel(tc, primary_input, prev, col, W0, b0, 
             stop=True,
         )
 
-        regroup(nc.scalar.copy, w1_grouped, w1_raw, row_pairs[0], lo)
+        regroup(nc.scalar.copy, w1_grouped, w1_raw, quarters[0])
         a0_rows = a_ps[0][:].rearrange("p (b t) -> p b t", t=T)
         h3_rows = h_planes[:, 3, :].rearrange("p (b t) -> p b t", t=T)
         nc.vector.tensor_scalar(
@@ -175,10 +173,9 @@ def tile_capsuleneuralnetwork_pa_s_kernel(tc, primary_input, prev, col, W0, b0, 
         )
         for c in (2, 3):
             nc.scalar.activation(out=h_planes[:, c - 1, :], in_=a_ps[c][:], func=RELU, bias=bias0[:, c : c + 1], scale=1.0)
-        regroup(nc.scalar.copy, w1_grouped, w1_raw, row_pairs[1], lo)
+        regroup(nc.scalar.copy, w1_grouped, w1_raw, quarters[1])
         nc.scalar.copy(out=bias1[:], in_=bias1_ps[:])
-        for rows in row_pairs:
-            regroup(nc.vector.tensor_copy, w1_grouped, w1_raw, rows, hi)
+        regroup(nc.vector.tensor_copy, w1_grouped, w1_raw, hi)
         nc.vector.tensor_copy(out=h_grouped[:], in_=h_planes[:].rearrange("p j r -> p r j"))
         quantise(nc, w1_codes[:, hi], w1_scales[:, hi], w1_grouped[:, hi, :])
         quantise(nc, h_codes[:], h_scales[:], h_grouped[:])

@@ -63,7 +63,8 @@ def tile_capsuleneuralnetwork_pa_s_kernel(tc, primary_input, prev, col, W0, b0, 
         h_codes = keep.tile([P, P], U32, align_bytes=64)
         h_scales = keep.tile([P, P], U8, align_bytes=64)
         ident = keep.tile([P, P], F32)
-        bias_rows = keep.tile([P, 2, WIDTH], BF16)
+        bias0_rows = keep.tile([P, WIDTH], BF16)
+        bias1_rows = keep.tile([P, WIDTH], BF16)
         weight_of_row = keep.tile([P, 1], BF16)
         bias0 = keep.tile([P, CHUNKS], F32)
         bias1 = keep.tile([P, WIDTH], F32)
@@ -76,15 +77,16 @@ def tile_capsuleneuralnetwork_pa_s_kernel(tc, primary_input, prev, col, W0, b0, 
         bias1_ps = psum.tile([P, WIDTH], F32)
         a_ps = [psum.tile([P, P], F32, name="a_ps%d" % c) for c in range(CHUNKS)]
 
-        nc.vector.memset(weight_of_row[:], 0.0)
-        nc.vector.memset(weight_of_row[0:1, :], 1.0)
-        nc.vector.memset(bias_rows[:], 0.0)
+        nc.gpsimd.memset(weight_of_row[:], 0.0)
+        nc.gpsimd.memset(weight_of_row[0:1, :], 1.0)
+        nc.gpsimd.memset(bias0_rows[:].bitcast(F32), 0.0)
         nc.vector.memset(warm[:], 0.0)
+        nc.vector.memset(bias1_rows[:], 0.0)
         make_identity(nc, ident[:])
 
         nc.scalar.dma_start(out=weight_of_row[1:2, :], in_=col.unsqueeze(0))
-        nc.scalar.dma_start(out=bias_rows[0:1, 0, :], in_=b0.unsqueeze(0))
-        nc.scalar.dma_start(out=bias_rows[1:2, 0, :], in_=W0[L1_PASSES * K_PASS : L1_PASSES * K_PASS + 1, :])
+        nc.scalar.dma_start(out=bias0_rows[0:1, :], in_=b0.unsqueeze(0))
+        nc.scalar.dma_start(out=bias0_rows[1:2, :], in_=W0[L1_PASSES * K_PASS : L1_PASSES * K_PASS + 1, :])
         nc.scalar.activation(out=warm[:], in_=warm[:], func=RELU)
 
         nc.sync.dma_start(out=x_sb[:, 0:K_PASS], in_=primary_input.rearrange("b (t k) -> (b t) k", k=K_PASS))
@@ -95,8 +97,8 @@ def tile_capsuleneuralnetwork_pa_s_kernel(tc, primary_input, prev, col, W0, b0, 
                 in_=W0[g * K_PASS : (g + 1) * K_PASS, :].rearrange("(p j) w -> p j w", j=PACK),
             )
         nc.sync.dma_start(out=w1_raw[:], in_=W1[0:K_PASS, :].rearrange("(j p) w -> p j w", p=P))
-        nc.sync.dma_start(out=bias_rows[0:1, 1, :], in_=b1.unsqueeze(0))
-        nc.sync.dma_start(out=bias_rows[1:2, 1, :], in_=W1[K_PASS : K_PASS + 1, :])
+        nc.sync.dma_start(out=bias1_rows[0:1, :], in_=b1.unsqueeze(0))
+        nc.sync.dma_start(out=bias1_rows[1:2, :], in_=W1[K_PASS : K_PASS + 1, :])
 
 
         x_words = x_sb[:].bitcast(F32).rearrange("r (g p u) -> r g u p", g=L1_PASSES, u=2)
@@ -141,7 +143,7 @@ def tile_capsuleneuralnetwork_pa_s_kernel(tc, primary_input, prev, col, W0, b0, 
         for c in range(CHUNKS):
             nc.tensor.matmul(
                 out=bias0_ps[:, c : c + 1],
-                lhsT=bias_rows[:, 0, c * P : (c + 1) * P],
+                lhsT=bias0_rows[:, c * P : (c + 1) * P],
                 rhs=weight_of_row[:],
                 start=True,
                 stop=True,
@@ -154,7 +156,7 @@ def tile_capsuleneuralnetwork_pa_s_kernel(tc, primary_input, prev, col, W0, b0, 
         nc.tensor.matmul(
             out=bias1_ps[:],
             lhsT=weight_of_row[:].to_broadcast([P, P]),
-            rhs=bias_rows[:, 1, :],
+            rhs=bias1_rows[:],
             start=True,
             stop=True,
         )

@@ -7,6 +7,7 @@ U32 = mybir.dt.uint32
 U8 = mybir.dt.uint8
 FP8X4 = mybir.dt.float8_e4m3fn_x4
 ADD = mybir.AluOpType.add
+MULT = mybir.AluOpType.mult
 MAX = mybir.AluOpType.max
 RELU = mybir.ActivationFunctionType.Relu
 
@@ -63,9 +64,10 @@ def tile_capsuleneuralnetwork_pa_s_kernel(tc, primary_input, prev, col, W0, b0, 
         h_codes = keep.tile([P, P], U32, align_bytes=64)
         h_scales = keep.tile([P, P], U8, align_bytes=64)
         ident = keep.tile([P, P], F32)
-        bias0_rows = keep.tile([P, WIDTH], BF16)
+        bias0_rows = keep.tile([P, P], BF16)
         bias1_rows = keep.tile([P, WIDTH], BF16)
-        weight_of_row = keep.tile([P, 1], BF16)
+        col_rows = keep.tile([P, 1], BF16)
+        weights = keep.tile([P, CHUNKS], BF16)
         bias0 = keep.tile([P, CHUNKS], F32)
         bias1 = keep.tile([P, WIDTH], F32)
         y_sum = keep.tile([P, WIDTH], F32)
@@ -77,28 +79,26 @@ def tile_capsuleneuralnetwork_pa_s_kernel(tc, primary_input, prev, col, W0, b0, 
         bias1_ps = psum.tile([P, WIDTH], F32)
         a_ps = [psum.tile([P, P], F32, name="a_ps%d" % c) for c in range(CHUNKS)]
 
-        nc.gpsimd.memset(weight_of_row[:], 0.0)
-        nc.gpsimd.memset(weight_of_row[0:1, :], 1.0)
+        nc.gpsimd.memset(col_rows[:], 0.0)
         nc.gpsimd.memset(bias0_rows[:].bitcast(F32), 0.0)
         nc.vector.memset(warm[:], 0.0)
         nc.vector.memset(bias1_rows[:], 0.0)
         make_identity(nc, ident[:])
 
-        nc.scalar.dma_start(out=weight_of_row[1:2, :], in_=col.unsqueeze(0))
-        nc.scalar.dma_start(out=bias0_rows[0:1, :], in_=b0.unsqueeze(0))
-        nc.scalar.dma_start(out=bias0_rows[1:2, :], in_=W0[L1_PASSES * K_PASS : L1_PASSES * K_PASS + 1, :])
         nc.scalar.activation(out=warm[:], in_=warm[:], func=RELU)
 
         nc.sync.dma_start(out=x_sb[:, 0:K_PASS], in_=primary_input.rearrange("b (t k) -> (b t) k", k=K_PASS))
         nc.sync.dma_start(out=x_sb[:, K_PASS : 2 * K_PASS], in_=prev.rearrange("b (t k) -> (b t) k", k=K_PASS))
-        for g in range(L1_PASSES):
-            nc.sync.dma_start(
-                out=w0_raw[:, g],
-                in_=W0[g * K_PASS : (g + 1) * K_PASS, :].rearrange("(p j) w -> p j w", j=PACK),
-            )
+        w0_rows = [W0[g * K_PASS : (g + 1) * K_PASS, :].rearrange("(p j) w -> p j w", j=PACK) for g in range(L1_PASSES)]
+        nc.sync.dma_start(out=w0_raw[:, 0], in_=w0_rows[0])
+        w0_last = W0[L1_PASSES * K_PASS : L1_PASSES * K_PASS + 1, :]
+        nc.sync.dma_start(out=bias0_rows[0:CHUNKS, :], in_=b0.rearrange("(c p) -> c p", p=P))
+        nc.sync.dma_start(out=bias0_rows[CHUNKS : 2 * CHUNKS, :], in_=w0_last.rearrange("o (c p) -> (o c) p", p=P))
+        nc.sync.dma_start(out=col_rows[CHUNKS : 2 * CHUNKS, :], in_=col.partition_broadcast(CHUNKS))
+        nc.sync.dma_start(out=w0_raw[:, 1], in_=w0_rows[1])
         nc.sync.dma_start(out=w1_raw[:], in_=W1[0:K_PASS, :].rearrange("(j p) w -> p j w", p=P))
         nc.sync.dma_start(out=bias1_rows[0:1, :], in_=b1.unsqueeze(0))
-        nc.sync.dma_start(out=bias1_rows[1:2, :], in_=W1[K_PASS : K_PASS + 1, :])
+        nc.sync.dma_start(out=bias1_rows[CHUNKS : CHUNKS + 1, :], in_=W1[K_PASS : K_PASS + 1, :])
 
 
         x_words = x_sb[:].bitcast(F32).rearrange("r (g p u) -> r g u p", g=L1_PASSES, u=2)
@@ -133,29 +133,30 @@ def tile_capsuleneuralnetwork_pa_s_kernel(tc, primary_input, prev, col, W0, b0, 
             scales=x_scales[:].rearrange("p g r -> p (g r)"),
             in_=x_grouped[:],
         )
+        nc.vector.scalar_tensor_tensor(
+            out=weights[:],
+            in0=ident[:, CHUNKS : 2 * CHUNKS],
+            scalar=col_rows[:],
+            in1=ident[:, 0:CHUNKS],
+            op0=MULT,
+            op1=ADD,
+        )
         quantise_w0(0, lo)
         layer1(0, (0, 1))
+        nc.tensor.matmul(out=bias0_ps[:], lhsT=bias0_rows[:], rhs=weights[:], start=True, stop=True)
         regroup(nc.vector.tensor_copy, w0_grouped[:, 1], w0_raw[:, 1], lo)
         regroup(nc.scalar.copy, w0_grouped[:, 1], w0_raw[:, 1], quarters[2])
         regroup(nc.scalar.copy, w0_grouped[:, 1], w0_raw[:, 1], quarters[3])
         quantise_w0(0, hi)
         layer1(0, (2, 3))
-        for c in range(CHUNKS):
-            nc.tensor.matmul(
-                out=bias0_ps[:, c : c + 1],
-                lhsT=bias0_rows[:, c * P : (c + 1) * P],
-                rhs=weight_of_row[:],
-                start=True,
-                stop=True,
-            )
+        nc.vector.tensor_copy(out=bias0[:], in_=bias0_ps[:])
         quantise_w0(1, lo)
         layer1(1, (0, 1))
         quantise_w0(1, hi)
         layer1(1, (2, 3))
-        nc.vector.tensor_copy(out=bias0[:], in_=bias0_ps[:])
         nc.tensor.matmul(
             out=bias1_ps[:],
-            lhsT=weight_of_row[:].to_broadcast([P, P]),
+            lhsT=weights[:, 0:1].to_broadcast([P, P]),
             rhs=bias1_rows[:],
             start=True,
             stop=True,

@@ -126,8 +126,7 @@ def tile_capsuleneuralnetwork_pa_s_kernel(tc, primary_input, prev, col, W0, b0, 
             quantise(nc, w0_codes[:, g, cols], w0_scales[:, g, cols], w0_grouped[:, g, cols, :])
 
         regroup(nc.vector.tensor_copy, w0_grouped[:, 0], w0_raw[:, 0], lo)
-        regroup(nc.scalar.copy, w0_grouped[:, 0], w0_raw[:, 0], quarters[2])
-        regroup(nc.scalar.copy, w0_grouped[:, 0], w0_raw[:, 0], quarters[3])
+        regroup(nc.scalar.copy, w0_grouped[:, 0], w0_raw[:, 0], hi)
         nc.vector.quantize_mx(
             out=x_codes[:].rearrange("p g r -> p (g r)").bitcast(FP8X4),
             scales=x_scales[:].rearrange("p g r -> p (g r)"),
@@ -152,8 +151,9 @@ def tile_capsuleneuralnetwork_pa_s_kernel(tc, primary_input, prev, col, W0, b0, 
         nc.vector.tensor_copy(out=bias0[:], in_=bias0_ps[:])
         quantise_w0(1, lo)
         layer1(1, (0, 1))
-        quantise_w0(1, hi)
-        layer1(1, (2, 3))
+        for q in (2, 3):
+            quantise_w0(1, quarters[q])
+            layer1(1, (q,))
         nc.tensor.matmul(
             out=bias1_ps[:],
             lhsT=weights[:, 0:1].to_broadcast([P, P]),

import concourse.mybir as mybir
from concourse.masks import make_identity

BF16 = mybir.dt.bfloat16
F32 = mybir.dt.float32
U32 = mybir.dt.uint32
U8 = mybir.dt.uint8
FP8X4 = mybir.dt.float8_e4m3fn_x4
ADD = mybir.AluOpType.add
MULT = mybir.AluOpType.mult
MAX = mybir.AluOpType.max
RELU = mybir.ActivationFunctionType.Relu

P = 128
PACK = 4
K_PASS = P * PACK
T = 8
WIDTH = 512
ROLL = 128
HALF = WIDTH // 2
QUARTER = WIDTH // 4
L1_PASSES = 2
CHUNKS = WIDTH // P

FLOPS = 2 * P * (L1_PASSES * K_PASS) * WIDTH + 2 * P * K_PASS * WIDTH


def regroup(copy, grouped, raw, cols):
    copy(
        out=grouped[:, cols, :].rearrange("p (c i) j -> p c j i", i=4),
        in_=raw[:, :, cols].rearrange("p j (c i) -> p c j i", i=4),
    )


def quantise(nc, codes, scales, grouped):
    nc.vector.quantize_mx(
        out=codes.bitcast(FP8X4),
        scales=scales,
        in_=grouped.rearrange("p w j -> p (w j)"),
    )


def tile_capsuleneuralnetwork_pa_s_kernel(tc, primary_input, prev, col, W0, b0, W1, b1, out):
    nc = tc.nc
    lo = slice(0, HALF)
    hi = slice(HALF, WIDTH)
    quarters = [slice(q * QUARTER, (q + 1) * QUARTER) for q in range(4)]

    with tc.tile_pool(name="keep", bufs=1) as keep, tc.psum_pool(name="psum", bufs=1) as psum, tc.manual_schedule():
        x_sb = keep.tile([P, L1_PASSES * K_PASS], BF16)
        x_grouped = keep.tile([P, L1_PASSES * P * PACK], BF16, align_bytes=64)
        x_codes = keep.tile([P, L1_PASSES, P], U32, align_bytes=64)
        x_scales = keep.tile([P, L1_PASSES, P], U8, align_bytes=64)
        w0_raw = keep.tile([P, L1_PASSES, PACK, WIDTH], BF16)
        w0_grouped = keep.tile([P, L1_PASSES, WIDTH, PACK], BF16, align_bytes=64)
        w0_codes = keep.tile([P, L1_PASSES, WIDTH], U32, align_bytes=64)
        w0_scales = keep.tile([P, L1_PASSES, WIDTH], U8, align_bytes=64)
        w1_raw = keep.tile([P, PACK, WIDTH], BF16)
        w1_grouped = keep.tile([P, WIDTH, PACK], BF16, align_bytes=64)
        w1_codes = keep.tile([P, WIDTH], U32, align_bytes=64)
        w1_scales = keep.tile([P, WIDTH], U8, align_bytes=64)
        h_planes = keep.tile([P, PACK, P], BF16)
        h_grouped = keep.tile([P, P, PACK], BF16, align_bytes=64)
        h_codes = keep.tile([P, P], U32, align_bytes=64)
        h_scales = keep.tile([P, P], U8, align_bytes=64)
        ident = keep.tile([P, P], F32)
        bias0_rows = keep.tile([P, P], BF16)
        bias1_rows = keep.tile([P, WIDTH], BF16)
        col_rows = keep.tile([P, 1], BF16)
        weights = keep.tile([P, CHUNKS], BF16)
        bias0 = keep.tile([P, CHUNKS], F32)
        bias1 = keep.tile([P, WIDTH], F32)
        y_sum = keep.tile([P, WIDTH], F32)
        y_out = keep.tile([P, WIDTH], F32)
        warm = keep.tile([P, 1], F32)

        xt = [psum.tile([P, 2, P], F32, name="xt%d" % g, tag="bank%d" % g) for g in range(L1_PASSES)]
        bias0_ps = psum.tile([P, CHUNKS], F32)
        bias1_ps = psum.tile([P, WIDTH], F32)
        a_ps = [psum.tile([P, P], F32, name="a_ps%d" % c) for c in range(CHUNKS)]

        nc.gpsimd.memset(col_rows[:], 0.0)
        nc.gpsimd.memset(bias0_rows[:].bitcast(F32), 0.0)
        nc.vector.memset(warm[:], 0.0)
        nc.vector.memset(bias1_rows[:], 0.0)
        make_identity(nc, ident[:])

        nc.scalar.activation(out=warm[:], in_=warm[:], func=RELU)

        nc.sync.dma_start(out=x_sb[:, 0:K_PASS], in_=primary_input.rearrange("b (t k) -> (b t) k", k=K_PASS))
        nc.sync.dma_start(out=x_sb[:, K_PASS : 2 * K_PASS], in_=prev.rearrange("b (t k) -> (b t) k", k=K_PASS))
        w0_rows = [W0[g * K_PASS : (g + 1) * K_PASS, :].rearrange("(p j) w -> p j w", j=PACK) for g in range(L1_PASSES)]
        nc.sync.dma_start(out=w0_raw[:, 0], in_=w0_rows[0])
        w0_last = W0[L1_PASSES * K_PASS : L1_PASSES * K_PASS + 1, :]
        nc.sync.dma_start(out=bias0_rows[0:CHUNKS, :], in_=b0.rearrange("(c p) -> c p", p=P))
        nc.sync.dma_start(out=bias0_rows[CHUNKS : 2 * CHUNKS, :], in_=w0_last.rearrange("o (c p) -> (o c) p", p=P))
        nc.sync.dma_start(out=col_rows[CHUNKS : 2 * CHUNKS, :], in_=col.partition_broadcast(CHUNKS))
        nc.sync.dma_start(out=w0_raw[:, 1], in_=w0_rows[1])
        nc.sync.dma_start(out=w1_raw[:], in_=W1[0:K_PASS, :].rearrange("(j p) w -> p j w", p=P))
        nc.sync.dma_start(out=bias1_rows[0:1, :], in_=b1.unsqueeze(0))
        nc.sync.dma_start(out=bias1_rows[CHUNKS : CHUNKS + 1, :], in_=W1[K_PASS : K_PASS + 1, :])


        x_words = x_sb[:].bitcast(F32).rearrange("r (g p u) -> r g u p", g=L1_PASSES, u=2)
        x_grouped_words = x_grouped[:].bitcast(F32).rearrange("p (g r u) -> p g r u", g=L1_PASSES, u=2)
        for g in range(L1_PASSES):
            for u in range(2):
                nc.tensor.transpose(out=xt[g][:, u, :], in_=x_words[:, g, u, :], identity=ident[:])
        nc.vector.tensor_copy(out=x_grouped_words[:, 0], in_=xt[0][:].rearrange("p u r -> p r u"))
        nc.scalar.copy(out=x_grouped_words[:, 1], in_=xt[1][:].rearrange("p u r -> p r u"))

        def layer1(g, chunks):
            for c in chunks:
                cols = slice(c * P, (c + 1) * P)
                nc.tensor.matmul_mx(
                    out=a_ps[c][:],
                    lhsT=w0_codes[:, g, cols].bitcast(FP8X4),
                    lhsT_scale=w0_scales[:, g, cols],
                    rhs=x_codes[:, g, :].bitcast(FP8X4),
                    rhs_scale=x_scales[:, g, :],
                    start=(g == 0),
                    stop=(g == L1_PASSES - 1),
                )

        def quantise_w0(g, cols):
            quantise(nc, w0_codes[:, g, cols], w0_scales[:, g, cols], w0_grouped[:, g, cols, :])

        regroup(nc.vector.tensor_copy, w0_grouped[:, 0], w0_raw[:, 0], lo)
        regroup(nc.scalar.copy, w0_grouped[:, 0], w0_raw[:, 0], hi)
        nc.vector.quantize_mx(
            out=x_codes[:].rearrange("p g r -> p (g r)").bitcast(FP8X4),
            scales=x_scales[:].rearrange("p g r -> p (g r)"),
            in_=x_grouped[:],
        )
        nc.vector.scalar_tensor_tensor(
            out=weights[:],
            in0=ident[:, CHUNKS : 2 * CHUNKS],
            scalar=col_rows[:],
            in1=ident[:, 0:CHUNKS],
            op0=MULT,
            op1=ADD,
        )
        quantise_w0(0, lo)
        layer1(0, (0, 1))
        nc.tensor.matmul(out=bias0_ps[:], lhsT=bias0_rows[:], rhs=weights[:], start=True, stop=True)
        regroup(nc.vector.tensor_copy, w0_grouped[:, 1], w0_raw[:, 1], lo)
        regroup(nc.scalar.copy, w0_grouped[:, 1], w0_raw[:, 1], quarters[2])
        regroup(nc.scalar.copy, w0_grouped[:, 1], w0_raw[:, 1], quarters[3])
        quantise_w0(0, hi)
        layer1(0, (2, 3))
        nc.vector.tensor_copy(out=bias0[:], in_=bias0_ps[:])
        quantise_w0(1, lo)
        layer1(1, (0, 1))
        for q in (2, 3):
            quantise_w0(1, quarters[q])
            layer1(1, (q,))
        nc.tensor.matmul(
            out=bias1_ps[:],
            lhsT=weights[:, 0:1].to_broadcast([P, P]),
            rhs=bias1_rows[:],
            start=True,
            stop=True,
        )

        regroup(nc.scalar.copy, w1_grouped, w1_raw, quarters[0])
        a0_rows = a_ps[0][:].rearrange("p (b t) -> p b t", t=T)
        h3_rows = h_planes[:, 3, :].rearrange("p (b t) -> p b t", t=T)
        nc.vector.tensor_scalar(
            out=h3_rows[:, :, 0 : T - 1], in0=a0_rows[:, :, 1:T], scalar1=bias0[:, 0:1], scalar2=0.0, op0=ADD, op1=MAX
        )
        nc.vector.tensor_scalar(
            out=h3_rows[:, :, T - 1 : T], in0=a0_rows[:, :, 0:1], scalar1=bias0[:, 0:1], scalar2=0.0, op0=ADD, op1=MAX
        )
        nc.vector.tensor_scalar(
            out=h_planes[:, 0, :], in0=a_ps[1][:], scalar1=bias0[:, 1:2], scalar2=0.0, op0=ADD, op1=MAX
        )
        for c in (2, 3):
            nc.scalar.activation(out=h_planes[:, c - 1, :], in_=a_ps[c][:], func=RELU, bias=bias0[:, c : c + 1], scale=1.0)
        regroup(nc.scalar.copy, w1_grouped, w1_raw, quarters[1])
        nc.scalar.copy(out=bias1[:], in_=bias1_ps[:])
        regroup(nc.vector.tensor_copy, w1_grouped, w1_raw, hi)
        nc.vector.tensor_copy(out=h_grouped[:], in_=h_planes[:].rearrange("p j r -> p r j"))
        quantise(nc, w1_codes[:, hi], w1_scales[:, hi], w1_grouped[:, hi, :])
        quantise(nc, h_codes[:], h_scales[:], h_grouped[:])
        quantise(nc, w1_codes[:, lo], w1_scales[:, lo], w1_grouped[:, lo, :])

        out_rows = out.rearrange("b (t f) -> (b t) f", f=WIDTH)
        y_ps = {}
        for n, cols in enumerate((hi, lo)):
            y_ps[n] = psum.tile([P, HALF], F32, name="y_ps%d" % n, tag="bank%d" % n)
            nc.tensor.matmul_mx(
                out=y_ps[n][:],
                lhsT=h_codes[:].bitcast(FP8X4),
                lhsT_scale=h_scales[:],
                rhs=w1_codes[:, cols].bitcast(FP8X4),
                rhs_scale=w1_scales[:, cols],
                start=True,
                stop=True,
            )
            nc.vector.tensor_tensor(out=y_sum[:, cols], in0=y_ps[n][:], in1=bias1[:, cols], op=ADD)
            nc.scalar.activation(out=y_out[:, cols], in_=y_sum[:, cols], func=RELU)
            if n == 0:
                last = slice(WIDTH - ROLL, WIDTH)
                for step in (2, 4, 8):
                    first = step // 2 - 1
                    nc.sync.dma_start(out=out_rows[first + 1 : P : step, 0:ROLL], in_=y_out[first:P:step, last])
                nc.sync.dma_start(out=out_rows[0:P:T, 0:ROLL], in_=y_out[T - 1 : P : T, last])
                nc.sync.dma_start(out=out_rows[:, HALF + ROLL : WIDTH], in_=y_out[:, HALF : WIDTH - ROLL])
            else:
                nc.scalar.dma_start(out=out_rows[:, ROLL : HALF + ROLL], in_=y_out[:, lo])
